import numpy as np
import ml_dtypes


def mxq(x, axis, fmt="e4m3"):
    dtype, down = {"e4m3": (ml_dtypes.float8_e4m3fn, 7), "e5m2": (ml_dtypes.float8_e5m2, 14)}[fmt]
    v = np.moveaxis(np.asarray(x, np.float32).astype(ml_dtypes.bfloat16).astype(np.float64), axis, -1)
    blocks = v.reshape(v.shape[:-1] + (-1, 32))
    amax = np.abs(blocks).max(-1, keepdims=True)
    byte = np.maximum(np.where(amax > 0, np.frexp(amax)[1] - 1 + 127, 0) - down, 1)
    scale = np.exp2(byte - 127.0)
    codes = (blocks / scale).astype(np.float32).astype(dtype).astype(np.float64)
    return np.moveaxis((codes * scale).reshape(v.shape), -1, axis)


WIDE = False


def mx_kscale(k):
    if not WIDE:
        return np.ones(k)
    levels = np.array([10, -10, 5, -5, 0])
    a = np.random.permutation(np.resize(levels, k // 512 * 4)).reshape(k // 512, 4)
    idx = np.arange(k)
    return np.exp2(a[idx // 512, idx % 128 // 32])


BF16 = ml_dtypes.bfloat16


def bf(x):
    return np.asarray(x, np.float32).astype(BF16)


def f64(x):
    return np.asarray(x).astype(np.float64)


B, T, C, H = 8, 512, 512, 4
DH = C // H


def rope_tables():
    i = f64(np.arange(1, DH // 2 + 1))
    thetas = np.repeat(1000.0 ** (-2.0 * i / DH), 2)
    pos = f64(np.arange(1, T + 1))
    args = pos[:, None] * thetas[None, :]
    return np.sin(args), np.cos(args)


def apply_rope(u, sin, cos):
    u_odd = u[..., ::2]
    u_even = u[..., 1::2]
    u_sin = np.stack([-u_even, u_odd], axis=-1).reshape(u.shape)
    return u * cos + u_sin * sin


def setup_inputs():
    s = mx_kscale(C)
    return {"x": bf(np.random.standard_normal((B, T, C)) * s),
            "w_qk": bf(np.random.standard_normal((2 * C, C)) / np.sqrt(C) / s[None, :])}


def reference(x, w_qk):
    qk = mxq(f64(x), 2, "e4m3") @ mxq(f64(w_qk), 1, "e4m3").T
    q, k = np.split(qk, 2, axis=-1)
    q = q.reshape(B, T, H, DH).transpose(0, 2, 1, 3)
    k = k.reshape(B, T, H, DH).transpose(0, 2, 1, 3)
    sin, cos = rope_tables()
    return q, k, apply_rope(q, sin, cos), apply_rope(k, sin, cos)

@@ -1,0 +1,259 @@
+import math
+from contextlib import ExitStack
+
+import concourse.mybir as mybir
+from concourse.masks import make_identity
+
+F32 = mybir.dt.float32
+BF16 = mybir.dt.bfloat16
+I32 = mybir.dt.int32
+U32 = mybir.dt.uint32
+U8 = mybir.dt.uint8
+FP8X4 = mybir.dt.float8_e4m3fn_x4
+ALU = mybir.AluOpType
+ACT = mybir.ActivationFunctionType
+
+P = 128
+BATCH, POSITIONS, CHANNELS, HEADS = 8, 512, 512, 4
+HEAD_DIM = CHANNELS // HEADS
+PAIRS = HEAD_DIM // 2
+WORDS = CHANNELS // 2
+HALF_TILES = CHANNELS // P
+SUB = POSITIONS // P
+
+FLOPS = 2 * BATCH * POSITIONS * CHANNELS * 2 * CHANNELS
+
+ROUND_MAGIC = 12582912.0
+
+
+def reduce_rotation_angles(nc, pool):
+    one = pool.tile([P, 1], F32)
+    nc.vector.memset(one[:], 1.0)
+    warm = pool.tile([P, 1], F32)
+    nc.scalar.activation(out=warm[:], in_=one[:], func=ACT.Sin)
+
+    position_int = pool.tile([P, SUB], I32)
+    nc.gpsimd.iota(position_int[:], pattern=[[1, SUB]], base=1, channel_multiplier=SUB)
+    position = pool.tile([P, SUB], F32)
+    nc.vector.tensor_copy(out=position[:], in_=position_int[:])
+
+    ratio = 1000.0 ** (-2.0 / HEAD_DIM)
+    frequency = pool.tile([P, PAIRS], F32)
+    nc.vector.tensor_scalar_mul(out=frequency[:, 0:1], in0=one[:], scalar1=ratio / (2.0 * math.pi))
+    half = 1
+    while half < PAIRS:
+        nc.vector.tensor_scalar_mul(
+            out=frequency[:, half : 2 * half], in0=frequency[:, 0:half], scalar1=ratio**half
+        )
+        half *= 2
+    plus_half_pi = pool.tile([P, 1], F32)
+    nc.vector.tensor_scalar_mul(out=plus_half_pi[:], in0=one[:], scalar1=0.5 * math.pi)
+    minus_half_pi = pool.tile([P, 1], F32)
+    nc.vector.tensor_scalar_mul(out=minus_half_pi[:], in0=one[:], scalar1=-0.5 * math.pi)
+
+    n = SUB * PAIRS
+    turns = pool.tile([P, 2, n], F32)
+    nc.vector.tensor_tensor(
+        out=turns[:, 0, :].rearrange("p (i j) -> p i j", j=PAIRS),
+        in0=position[:].unsqueeze(2).to_broadcast([P, SUB, PAIRS]),
+        in1=frequency[:].unsqueeze(1).to_broadcast([P, SUB, PAIRS]),
+        op=ALU.mult,
+    )
+    nc.vector.tensor_scalar_add(out=turns[:, 1, :], in0=turns[:, 0, :], scalar1=-0.25)
+    whole = pool.tile([P, 2, n], F32)
+    nc.vector.tensor_scalar(
+        out=whole[:],
+        in0=turns[:],
+        scalar1=ROUND_MAGIC,
+        scalar2=ROUND_MAGIC,
+        op0=ALU.add,
+        op1=ALU.subtract,
+    )
+    part = pool.tile([P, 2, n], F32)
+    nc.vector.tensor_tensor(out=part[:], in0=turns[:], in1=whole[:], op=ALU.subtract)
+    size = pool.tile([P, 2, n], F32)
+    nc.vector.scalar_tensor_tensor(
+        out=size[:], in0=part[:], scalar=-1.0, in1=part[:], op0=ALU.mult, op1=ALU.max
+    )
+    return size, plus_half_pi, minus_half_pi
+
+
+def fill_rotation_tables(nc, size, plus_half_pi, minus_half_pi, cos_table, sin_table):
+    n = SUB * PAIRS
+    cos_pairs = cos_table.rearrange("p i (j e) -> p (i j) e", e=2)
+    sin_pairs = sin_table.rearrange("p i (j e) -> p (i j) e", e=2)
+    nc.scalar.activation(
+        out=sin_pairs[:, :, 0:1],
+        in_=size[:, 1, :].unsqueeze(2),
+        func=ACT.Sin,
+        bias=minus_half_pi[:],
+        scale=2.0 * math.pi,
+    )
+    nc.scalar.activation(
+        out=sin_pairs[:, :, 1:2],
+        in_=size[:, 1, :].unsqueeze(2),
+        func=ACT.Sin,
+        bias=plus_half_pi[:],
+        scale=-2.0 * math.pi,
+    )
+    nc.scalar.activation(
+        out=cos_pairs,
+        in_=size[:, 0, :].unsqueeze(2).to_broadcast([P, n, 2]),
+        func=ACT.Sin,
+        bias=plus_half_pi[:],
+        scale=-2.0 * math.pi,
+    )
+
+
+def channels_to_partitions(nc, banks, rows, n_tiles, permutation, grouped):
+    words = rows.bitcast(F32)
+    grouped_words = grouped.bitcast(F32).rearrange("p (t r u) -> p t r u", r=P, u=2)
+    for first in range(0, n_tiles, 2):
+        bank = banks.tile([P, 2, 2, P], F32, tag="transposed")
+        for t in range(2):
+            for u in range(2):
+                start = (first + t) * WORDS + u * P
+                nc.tensor.transpose(bank[:, t, u, :], words[:, start : start + P], permutation)
+        nc.scalar.copy(
+            out=grouped_words[:, first : first + 2, :, :],
+            in_=bank[:].rearrange("p t u r -> p t r u"),
+        )
+
+
+def tile_ropeattnlayer_pa_t_kernel(tc, x, w_qk, out_0, out_1, out_2, out_3):
+    nc = tc.nc
+    raw_outs = (out_0, out_1)
+    rotated_outs = (out_2, out_3)
+
+    with ExitStack() as ctx:
+        keep = ctx.enter_context(tc.tile_pool(name="keep", bufs=1))
+        stage = ctx.enter_context(tc.tile_pool(name="stage", bufs=2))
+        terms = ctx.enter_context(tc.tile_pool(name="terms", bufs=3))
+        results = ctx.enter_context(tc.tile_pool(name="results", bufs=4))
+        banks = ctx.enter_context(tc.psum_pool(name="banks", bufs=2))
+        sums = ctx.enter_context(tc.psum_pool(name="sums", bufs=6))
+        ctx.enter_context(tc.manual_schedule())
+
+        x_rows = []
+        for b in range(BATCH):
+            x_rows.append(keep.tile([P, SUB * CHANNELS], BF16, name="x_rows_%d" % b))
+        w_rows = []
+        for s in range(2):
+            w_rows.append(keep.tile([P, HALF_TILES * CHANNELS], BF16, name="w_rows_%d" % s))
+
+        def load_x(b):
+            nc.sync.dma_start(out=x_rows[b][:], in_=x[b].rearrange("(p i) c -> p (i c)", i=SUB))
+
+        def load_w(s):
+            nc.sync.dma_start(
+                out=w_rows[s][:].rearrange("p (t c) -> p t c", c=CHANNELS),
+                in_=w_qk[s * CHANNELS : (s + 1) * CHANNELS, :].rearrange("(t p) c -> p t c", p=P),
+            )
+
+        load_x(0)
+        load_w(0)
+        for b in range(1, BATCH):
+            load_x(b)
+        load_w(1)
+
+        identity = keep.tile([P, P], F32)
+        make_identity(nc, identity[:])
+        swap = keep.tile([P, P], F32)
+        identity_pairs = identity[:].rearrange("p (m s) -> p m s", s=2)
+        swap_pairs = swap[:].rearrange("p (m s) -> p m s", s=2)
+        nc.vector.tensor_copy(out=swap_pairs[:, :, 0:1], in_=identity_pairs[:, :, 1:2])
+        nc.vector.tensor_copy(out=swap_pairs[:, :, 1:2], in_=identity_pairs[:, :, 0:1])
+
+        size, plus_half_pi, minus_half_pi = reduce_rotation_angles(nc, keep)
+
+        x_codes = []
+        x_scales = []
+        for b in range(BATCH):
+            x_codes.append(keep.tile([P, POSITIONS], U32, name="x_codes_%d" % b, align_bytes=64))
+            x_scales.append(keep.tile([P, POSITIONS], U8, name="x_scales_%d" % b, align_bytes=64))
+
+        def group_x(b):
+            x_grouped = stage.tile([P, POSITIONS * 4], BF16, name="x_grouped", align_bytes=64)
+            channels_to_partitions(nc, banks, x_rows[b][:], SUB, identity[:], x_grouped[:])
+            return x_grouped
+
+        def quantise_x(b, x_grouped):
+            nc.vector.quantize_mx(
+                out=x_codes[b][:].bitcast(FP8X4), scales=x_scales[b][:], in_=x_grouped[:]
+            )
+
+        quantise_x(0, group_x(0))
+
+        cos_table = keep.tile([P, SUB, HEAD_DIM], F32)
+        sin_table = keep.tile([P, SUB, HEAD_DIM], F32)
+
+        for s in range(2):
+            w_codes = {}
+            w_scales = {}
+            for kind, permutation in (("partner", swap), ("own", identity)):
+                w_grouped = stage.tile([P, CHANNELS * 4], BF16, name="w_grouped", align_bytes=64)
+                w_codes[kind] = stage.tile([P, CHANNELS], U32, name="w_codes_" + kind, align_bytes=64)
+                w_scales[kind] = stage.tile([P, CHANNELS], U8, name="w_scales_" + kind, align_bytes=64)
+                channels_to_partitions(nc, banks, w_rows[s][:], HALF_TILES, permutation[:], w_grouped[:])
+                nc.vector.quantize_mx(
+                    out=w_codes[kind][:].bitcast(FP8X4), scales=w_scales[kind][:], in_=w_grouped[:]
+                )
+            if s == 0:
+                fill_rotation_tables(
+                    nc, size, plus_half_pi, minus_half_pi, cos_table[:], sin_table[:]
+                )
+
+            for b in range(BATCH):
+                quantise_next = s == 0 and b + 1 < BATCH
+                raw = results.tile([P, HEADS, SUB, HEAD_DIM], F32, name="raw")
+                rotated = results.tile([P, HEADS, SUB, HEAD_DIM], F32, name="rotated")
+                for first in range(0, SUB, 2):
+                    product = {}
+                    for kind in ("partner", "own"):
+                        for i in (first, first + 1):
+                            tokens = slice(i * P, (i + 1) * P)
+                            product[kind, i] = sums.tile([P, HEADS, HEAD_DIM], F32, name="product")
+                            nc.tensor.matmul_mx(
+                                out=product[kind, i][:].rearrange("p h f -> p (h f)"),
+                                lhsT=x_codes[b][:, tokens].bitcast(FP8X4),
+                                lhsT_scale=x_scales[b][:, tokens],
+                                rhs=w_codes[kind][:].bitcast(FP8X4),
+                                rhs_scale=w_scales[kind][:],
+                                start=True,
+                                stop=True,
+                            )
+                    if quantise_next and first == 0:
+                        x_grouped = group_x(b + 1)
+                    straight = terms.tile([P, 2, HEADS, HEAD_DIM], F32, name="straight")
+                    crossed = terms.tile([P, 2, HEADS, HEAD_DIM], F32, name="crossed")
+                    for i in (first, first + 1):
+                        nc.vector.tensor_tensor(
+                            out=crossed[:, i - first, :, :],
+                            in0=product["partner", i][:],
+                            in1=sin_table[:, i : i + 1, :].to_broadcast([P, HEADS, HEAD_DIM]),
+                            op=ALU.mult,
+                        )
+                    for i in (first, first + 1):
+                        nc.vector.tensor_tensor(
+                            out=straight[:, i - first, :, :],
+                            in0=product["own", i][:],
+                            in1=cos_table[:, i : i + 1, :].to_broadcast([P, HEADS, HEAD_DIM]),
+                            op=ALU.mult,
+                        )
+                        nc.scalar.copy(out=raw[:, :, i, :], in_=product["own", i][:])
+                    nc.gpsimd.tensor_tensor(
+                        out=rotated[:, :, first : first + 2, :],
+                        in0=straight[:].rearrange("p i h f -> p h i f"),
+                        in1=crossed[:].rearrange("p i h f -> p h i f"),
+                        op=ALU.add,
+                    )
+                    if quantise_next and first == 0:
+                        quantise_x(b + 1, x_grouped)
+                nc.scalar.dma_start(
+                    out=raw_outs[s][b].rearrange("h (p i) f -> p h (i f)", i=SUB),
+                    in_=raw[:].rearrange("p h i f -> p h (i f)"),
+                )
+                nc.sync.dma_start(
+                    out=rotated_outs[s][b].rearrange("h (p i) f -> p h (i f)", i=SUB),
+                    in_=rotated[:].rearrange("p h i f -> p h (i f)"),
+                )

@@ -166,45 +166,41 @@ def tile_ropeattnlayer_pa_t_kernel(tc, x, w_qk, out_0, out_1, out_2, out_3):
 
         size, plus_half_pi, minus_half_pi = reduce_rotation_angles(nc, keep)
 
-        x_codes = []
-        x_scales = []
-        for b in range(BATCH):
-            x_codes.append(keep.tile([P, POSITIONS], U32, name="x_codes_%d" % b, align_bytes=64))
-            x_scales.append(keep.tile([P, POSITIONS], U8, name="x_scales_%d" % b, align_bytes=64))
+        x_codes = {}
+        x_scales = {}
+        w_codes = {}
+        w_scales = {}
 
         def group_x(b):
             x_grouped = stage.tile([P, POSITIONS * 4], BF16, name="x_grouped", align_bytes=64)
+            x_codes[b] = keep.tile([P, POSITIONS], U32, name="x_codes_%d" % b, align_bytes=64)
+            x_scales[b] = keep.tile([P, POSITIONS], U8, name="x_scales_%d" % b, align_bytes=64)
             channels_to_partitions(nc, banks, x_rows[b][:], SUB, identity[:], x_grouped[:])
-            return x_grouped
+            return [(x_grouped, x_codes[b], x_scales[b])]
 
-        def quantise_x(b, x_grouped):
-            nc.vector.quantize_mx(
-                out=x_codes[b][:].bitcast(FP8X4), scales=x_scales[b][:], in_=x_grouped[:]
-            )
+        def group_w(s):
+            grouped = []
+            for kind, permutation in (("partner", swap), ("own", identity)):
+                label = "%s_%d" % (kind, s)
+                w_grouped = stage.tile([P, CHANNELS * 4], BF16, name="w_grouped", align_bytes=64)
+                w_codes[kind, s] = keep.tile([P, CHANNELS], U32, name="w_codes_" + label, align_bytes=64)
+                w_scales[kind, s] = keep.tile([P, CHANNELS], U8, name="w_scales_" + label, align_bytes=64)
+                channels_to_partitions(nc, banks, w_rows[s][:], HALF_TILES, permutation[:], w_grouped[:])
+                grouped.append((w_grouped, w_codes[kind, s], w_scales[kind, s]))
+            return grouped
 
-        quantise_x(0, group_x(0))
+        def quantise(grouped):
+            for values, codes, scales in grouped:
+                nc.vector.quantize_mx(out=codes[:].bitcast(FP8X4), scales=scales[:], in_=values[:])
+
+        quantise(group_x(0) + group_w(0))
 
         cos_table = keep.tile([P, SUB, HEAD_DIM], F32)
         sin_table = keep.tile([P, SUB, HEAD_DIM], F32)
+        fill_rotation_tables(nc, size, plus_half_pi, minus_half_pi, cos_table[:], sin_table[:])
 
         for s in range(2):
-            w_codes = {}
-            w_scales = {}
-            for kind, permutation in (("partner", swap), ("own", identity)):
-                w_grouped = stage.tile([P, CHANNELS * 4], BF16, name="w_grouped", align_bytes=64)
-                w_codes[kind] = stage.tile([P, CHANNELS], U32, name="w_codes_" + kind, align_bytes=64)
-                w_scales[kind] = stage.tile([P, CHANNELS], U8, name="w_scales_" + kind, align_bytes=64)
-                channels_to_partitions(nc, banks, w_rows[s][:], HALF_TILES, permutation[:], w_grouped[:])
-                nc.vector.quantize_mx(
-                    out=w_codes[kind][:].bitcast(FP8X4), scales=w_scales[kind][:], in_=w_grouped[:]
-                )
-            if s == 0:
-                fill_rotation_tables(
-                    nc, size, plus_half_pi, minus_half_pi, cos_table[:], sin_table[:]
-                )
-
             for b in range(BATCH):
-                quantise_next = s == 0 and b + 1 < BATCH
                 raw = results.tile([P, HEADS, SUB, HEAD_DIM], F32, name="raw")
                 rotated = results.tile([P, HEADS, SUB, HEAD_DIM], F32, name="rotated")
                 for first in range(0, SUB, 2):
@@ -217,16 +213,18 @@ def tile_ropeattnlayer_pa_t_kernel(tc, x, w_qk, out_0, out_1, out_2, out_3):
                                 out=product[kind, i][:].rearrange("p h f -> p (h f)"),
                                 lhsT=x_codes[b][:, tokens].bitcast(FP8X4),
                                 lhsT_scale=x_scales[b][:, tokens],
-                                rhs=w_codes[kind][:].bitcast(FP8X4),
-                                rhs_scale=w_scales[kind][:],
+                                rhs=w_codes[kind, s][:].bitcast(FP8X4),
+                                rhs_scale=w_scales[kind, s][:],
                                 start=True,
                                 stop=True,
                             )
-                    if quantise_next and first == 0:
-                        x_grouped = group_x(b + 1)
+                    grouped = []
+                    if s == 0 and first == 0:
+                        grouped = group_x(b + 1) if b + 1 < BATCH else group_w(1)
                     straight = terms.tile([P, 2, HEADS, HEAD_DIM], F32, name="straight")
                     crossed = terms.tile([P, 2, HEADS, HEAD_DIM], F32, name="crossed")
                     for i in (first, first + 1):
+                        nc.scalar.copy(out=raw[:, :, i, :], in_=product["own", i][:])
                         nc.vector.tensor_tensor(
                             out=crossed[:, i - first, :, :],
                             in0=product["partner", i][:],
@@ -240,15 +238,13 @@ def tile_ropeattnlayer_pa_t_kernel(tc, x, w_qk, out_0, out_1, out_2, out_3):
                             in1=cos_table[:, i : i + 1, :].to_broadcast([P, HEADS, HEAD_DIM]),
                             op=ALU.mult,
                         )
-                        nc.scalar.copy(out=raw[:, :, i, :], in_=product["own", i][:])
                     nc.gpsimd.tensor_tensor(
                         out=rotated[:, :, first : first + 2, :],
                         in0=straight[:].rearrange("p i h f -> p h i f"),
                         in1=crossed[:].rearrange("p i h f -> p h i f"),
                         op=ALU.add,
                     )
-                    if quantise_next and first == 0:
-                        quantise_x(b + 1, x_grouped)
+                    quantise(grouped)
                 nc.scalar.dma_start(
                     out=raw_outs[s][b].rearrange("h (p i) f -> p h (i f)", i=SUB),
                     in_=raw[:].rearrange("p h i f -> p h (i f)"),

@@ -201,6 +201,9 @@ def tile_ropeattnlayer_pa_t_kernel(tc, x, w_qk, out_0, out_1, out_2, out_3):
 
         for s in range(2):
             for b in range(BATCH):
+                grouped = []
+                if s == 0:
+                    grouped = group_x(b + 1) if b + 1 < BATCH else group_w(1)
                 raw = results.tile([P, HEADS, SUB, HEAD_DIM], F32, name="raw")
                 rotated = results.tile([P, HEADS, SUB, HEAD_DIM], F32, name="rotated")
                 for first in range(0, SUB, 2):
@@ -218,9 +221,6 @@ def tile_ropeattnlayer_pa_t_kernel(tc, x, w_qk, out_0, out_1, out_2, out_3):
                                 start=True,
                                 stop=True,
                             )
-                    grouped = []
-                    if s == 0 and first == 0:
-                        grouped = group_x(b + 1) if b + 1 < BATCH else group_w(1)
                     straight = terms.tile([P, 2, HEADS, HEAD_DIM], F32, name="straight")
                     crossed = terms.tile([P, 2, HEADS, HEAD_DIM], F32, name="crossed")
                     for i in (first, first + 1):
@@ -244,8 +244,9 @@ def tile_ropeattnlayer_pa_t_kernel(tc, x, w_qk, out_0, out_1, out_2, out_3):
                         in1=crossed[:].rearrange("p i h f -> p h i f"),
                         op=ALU.add,
                     )
-                    quantise(grouped)
-                nc.scalar.dma_start(
+                    if first == 0:
+                        quantise(grouped)
+                nc.sync.dma_start(
                     out=raw_outs[s][b].rearrange("h (p i) f -> p h (i f)", i=SUB),
                     in_=raw[:].rearrange("p h i f -> p h (i f)"),
                 )

@@ -199,6 +199,13 @@ def tile_ropeattnlayer_pa_t_kernel(tc, x, w_qk, out_0, out_1, out_2, out_3):
         sin_table = keep.tile([P, SUB, HEAD_DIM], F32)
         fill_rotation_tables(nc, size, plus_half_pi, minus_half_pi, cos_table[:], sin_table[:])
 
+        def store(outs, s, b, result):
+            nc.sync.dma_start(
+                out=outs[s][b].rearrange("h (p i) f -> p h (i f)", i=SUB),
+                in_=result[:].rearrange("p h i f -> p h (i f)"),
+            )
+
+        unstored = []
         for s in range(2):
             for b in range(BATCH):
                 grouped = []
@@ -206,6 +213,8 @@ def tile_ropeattnlayer_pa_t_kernel(tc, x, w_qk, out_0, out_1, out_2, out_3):
                     grouped = group_x(b + 1) if b + 1 < BATCH else group_w(1)
                 raw = results.tile([P, HEADS, SUB, HEAD_DIM], F32, name="raw")
                 rotated = results.tile([P, HEADS, SUB, HEAD_DIM], F32, name="rotated")
+                straight = terms.tile([P, SUB, HEADS, HEAD_DIM], F32, name="straight")
+                crossed = terms.tile([P, SUB, HEADS, HEAD_DIM], F32, name="crossed")
                 for first in range(0, SUB, 2):
                     product = {}
                     for kind in ("partner", "own"):
@@ -221,36 +230,34 @@ def tile_ropeattnlayer_pa_t_kernel(tc, x, w_qk, out_0, out_1, out_2, out_3):
                                 start=True,
                                 stop=True,
                             )
-                    straight = terms.tile([P, 2, HEADS, HEAD_DIM], F32, name="straight")
-                    crossed = terms.tile([P, 2, HEADS, HEAD_DIM], F32, name="crossed")
                     for i in (first, first + 1):
                         nc.scalar.copy(out=raw[:, :, i, :], in_=product["own", i][:])
                         nc.vector.tensor_tensor(
-                            out=crossed[:, i - first, :, :],
+                            out=crossed[:, i, :, :],
                             in0=product["partner", i][:],
                             in1=sin_table[:, i : i + 1, :].to_broadcast([P, HEADS, HEAD_DIM]),
                             op=ALU.mult,
                         )
                     for i in (first, first + 1):
                         nc.vector.tensor_tensor(
-                            out=straight[:, i - first, :, :],
+                            out=straight[:, i, :, :],
                             in0=product["own", i][:],
                             in1=cos_table[:, i : i + 1, :].to_broadcast([P, HEADS, HEAD_DIM]),
                             op=ALU.mult,
                         )
-                    nc.gpsimd.tensor_tensor(
-                        out=rotated[:, :, first : first + 2, :],
-                        in0=straight[:].rearrange("p i h f -> p h i f"),
-                        in1=crossed[:].rearrange("p i h f -> p h i f"),
-                        op=ALU.add,
-                    )
                     if first == 0:
                         quantise(grouped)
-                nc.sync.dma_start(
-                    out=raw_outs[s][b].rearrange("h (p i) f -> p h (i f)", i=SUB),
-                    in_=raw[:].rearrange("p h i f -> p h (i f)"),
+                last_step = s == 1 and b == BATCH - 1
+                adder = nc.vector if last_step else nc.gpsimd
+                adder.tensor_tensor(
+                    out=rotated[:],
+                    in0=straight[:].rearrange("p i h f -> p h i f"),
+                    in1=crossed[:].rearrange("p i h f -> p h i f"),
+                    op=ALU.add,
                 )
-                nc.sync.dma_start(
-                    out=rotated_outs[s][b].rearrange("h (p i) f -> p h (i f)", i=SUB),
-                    in_=rotated[:].rearrange("p h i f -> p h (i f)"),
-                )
+                store(raw_outs, s, b, raw)
+                for earlier in unstored:
+                    store(rotated_outs, *earlier)
+                unstored = [(s, b, rotated)]
+        for earlier in unstored:
+            store(rotated_outs, *earlier)

@@ -105,16 +105,17 @@ def fill_rotation_tables(nc, size, plus_half_pi, minus_half_pi, cos_table, sin_t
     )
 
 
-def channels_to_partitions(nc, banks, rows, n_tiles, permutation, grouped):
+def channels_to_partitions(nc, banks, copiers, rows, n_tiles, permutation, grouped):
     words = rows.bitcast(F32)
     grouped_words = grouped.bitcast(F32).rearrange("p (t r u) -> p t r u", r=P, u=2)
     for first in range(0, n_tiles, 2):
-        bank = banks.tile([P, 2, 2, P], F32, tag="transposed")
+        bank = banks.tile([P, 2, 2, P], F32, tag="bank")
         for t in range(2):
             for u in range(2):
                 start = (first + t) * WORDS + u * P
                 nc.tensor.transpose(bank[:, t, u, :], words[:, start : start + P], permutation)
-        nc.scalar.copy(
+        copy_out = copiers[(first // 2) % len(copiers)]
+        copy_out(
             out=grouped_words[:, first : first + 2, :, :],
             in_=bank[:].rearrange("p t u r -> p t r u"),
         )
@@ -130,31 +131,22 @@ def tile_ropeattnlayer_pa_t_kernel(tc, x, w_qk, out_0, out_1, out_2, out_3):
         stage = ctx.enter_context(tc.tile_pool(name="stage", bufs=2))
         terms = ctx.enter_context(tc.tile_pool(name="terms", bufs=3))
         results = ctx.enter_context(tc.tile_pool(name="results", bufs=4))
-        banks = ctx.enter_context(tc.psum_pool(name="banks", bufs=2))
-        sums = ctx.enter_context(tc.psum_pool(name="sums", bufs=6))
+        banks = ctx.enter_context(tc.psum_pool(name="banks", bufs=8))
         ctx.enter_context(tc.manual_schedule())
 
-        x_rows = []
-        for b in range(BATCH):
-            x_rows.append(keep.tile([P, SUB * CHANNELS], BF16, name="x_rows_%d" % b))
         w_rows = []
         for s in range(2):
             w_rows.append(keep.tile([P, HALF_TILES * CHANNELS], BF16, name="w_rows_%d" % s))
-
-        def load_x(b):
-            nc.sync.dma_start(out=x_rows[b][:], in_=x[b].rearrange("(p i) c -> p (i c)", i=SUB))
-
-        def load_w(s):
             nc.sync.dma_start(
                 out=w_rows[s][:].rearrange("p (t c) -> p t c", c=CHANNELS),
                 in_=w_qk[s * CHANNELS : (s + 1) * CHANNELS, :].rearrange("(t p) c -> p t c", p=P),
             )
+        x_rows = []
+        for b in range(BATCH):
+            x_rows.append(keep.tile([P, SUB * CHANNELS], BF16, name="x_rows_%d" % b))
+            nc.sync.dma_start(out=x_rows[b][:], in_=x[b].rearrange("(p i) c -> p (i c)", i=SUB))
 
-        load_x(0)
-        load_w(0)
-        for b in range(1, BATCH):
-            load_x(b)
-        load_w(1)
+        size, plus_half_pi, minus_half_pi = reduce_rotation_angles(nc, keep)
 
         identity = keep.tile([P, P], F32)
         make_identity(nc, identity[:])
@@ -164,36 +156,33 @@ def tile_ropeattnlayer_pa_t_kernel(tc, x, w_qk, out_0, out_1, out_2, out_3):
         nc.vector.tensor_copy(out=swap_pairs[:, :, 0:1], in_=identity_pairs[:, :, 1:2])
         nc.vector.tensor_copy(out=swap_pairs[:, :, 1:2], in_=identity_pairs[:, :, 0:1])
 
-        size, plus_half_pi, minus_half_pi = reduce_rotation_angles(nc, keep)
-
-        x_codes = {}
-        x_scales = {}
         w_codes = {}
         w_scales = {}
-
-        def group_x(b):
-            x_grouped = stage.tile([P, POSITIONS * 4], BF16, name="x_grouped", align_bytes=64)
-            x_codes[b] = keep.tile([P, POSITIONS], U32, name="x_codes_%d" % b, align_bytes=64)
-            x_scales[b] = keep.tile([P, POSITIONS], U8, name="x_scales_%d" % b, align_bytes=64)
-            channels_to_partitions(nc, banks, x_rows[b][:], SUB, identity[:], x_grouped[:])
-            return [(x_grouped, x_codes[b], x_scales[b])]
-
-        def group_w(s):
-            grouped = []
+        for s in range(2):
             for kind, permutation in (("partner", swap), ("own", identity)):
                 label = "%s_%d" % (kind, s)
                 w_grouped = stage.tile([P, CHANNELS * 4], BF16, name="w_grouped", align_bytes=64)
                 w_codes[kind, s] = keep.tile([P, CHANNELS], U32, name="w_codes_" + label, align_bytes=64)
                 w_scales[kind, s] = keep.tile([P, CHANNELS], U8, name="w_scales_" + label, align_bytes=64)
-                channels_to_partitions(nc, banks, w_rows[s][:], HALF_TILES, permutation[:], w_grouped[:])
-                grouped.append((w_grouped, w_codes[kind, s], w_scales[kind, s]))
-            return grouped
-
-        def quantise(grouped):
-            for values, codes, scales in grouped:
-                nc.vector.quantize_mx(out=codes[:].bitcast(FP8X4), scales=scales[:], in_=values[:])
-
-        quantise(group_x(0) + group_w(0))
+                channels_to_partitions(
+                    nc, banks, (nc.scalar.copy, nc.vector.tensor_copy),
+                    w_rows[s][:], HALF_TILES, permutation[:], w_grouped[:],
+                )
+                nc.vector.quantize_mx(
+                    out=w_codes[kind, s][:].bitcast(FP8X4), scales=w_scales[kind, s][:], in_=w_grouped[:]
+                )
+        x_codes = []
+        x_scales = []
+        for b in range(BATCH):
+            x_grouped = stage.tile([P, POSITIONS * 4], BF16, name="x_grouped", align_bytes=64)
+            x_codes.append(keep.tile([P, POSITIONS], U32, name="x_codes_%d" % b, align_bytes=64))
+            x_scales.append(keep.tile([P, POSITIONS], U8, name="x_scales_%d" % b, align_bytes=64))
+            channels_to_partitions(
+                nc, banks, (nc.scalar.copy,), x_rows[b][:], SUB, identity[:], x_grouped[:]
+            )
+            nc.vector.quantize_mx(
+                out=x_codes[b][:].bitcast(FP8X4), scales=x_scales[b][:], in_=x_grouped[:]
+            )
 
         cos_table = keep.tile([P, SUB, HEAD_DIM], F32)
         sin_table = keep.tile([P, SUB, HEAD_DIM], F32)
@@ -208,9 +197,6 @@ def tile_ropeattnlayer_pa_t_kernel(tc, x, w_qk, out_0, out_1, out_2, out_3):
         unstored = []
         for s in range(2):
             for b in range(BATCH):
-                grouped = []
-                if s == 0:
-                    grouped = group_x(b + 1) if b + 1 < BATCH else group_w(1)
                 raw = results.tile([P, HEADS, SUB, HEAD_DIM], F32, name="raw")
                 rotated = results.tile([P, HEADS, SUB, HEAD_DIM], F32, name="rotated")
                 straight = terms.tile([P, SUB, HEADS, HEAD_DIM], F32, name="straight")
@@ -220,7 +206,7 @@ def tile_ropeattnlayer_pa_t_kernel(tc, x, w_qk, out_0, out_1, out_2, out_3):
                     for kind in ("partner", "own"):
                         for i in (first, first + 1):
                             tokens = slice(i * P, (i + 1) * P)
-                            product[kind, i] = sums.tile([P, HEADS, HEAD_DIM], F32, name="product")
+                            product[kind, i] = banks.tile([P, HEADS, HEAD_DIM], F32, tag="bank", name="product")
                             nc.tensor.matmul_mx(
                                 out=product[kind, i][:].rearrange("p h f -> p (h f)"),
                                 lhsT=x_codes[b][:, tokens].bitcast(FP8X4),
@@ -245,8 +231,6 @@ def tile_ropeattnlayer_pa_t_kernel(tc, x, w_qk, out_0, out_1, out_2, out_3):
                             in1=cos_table[:, i : i + 1, :].to_broadcast([P, HEADS, HEAD_DIM]),
                             op=ALU.mult,
                         )
-                    if first == 0:
-                        quantise(grouped)
                 last_step = s == 1 and b == BATCH - 1
                 adder = nc.vector if last_step else nc.gpsimd
                 adder.tensor_tensor(

import math
from contextlib import ExitStack

import concourse.mybir as mybir
from concourse.masks import make_identity

F32 = mybir.dt.float32
BF16 = mybir.dt.bfloat16
I32 = mybir.dt.int32
U32 = mybir.dt.uint32
U8 = mybir.dt.uint8
FP8X4 = mybir.dt.float8_e4m3fn_x4
ALU = mybir.AluOpType
ACT = mybir.ActivationFunctionType

P = 128
BATCH, POSITIONS, CHANNELS, HEADS = 8, 512, 512, 4
HEAD_DIM = CHANNELS // HEADS
PAIRS = HEAD_DIM // 2
WORDS = CHANNELS // 2
HALF_TILES = CHANNELS // P
SUB = POSITIONS // P

FLOPS = 2 * BATCH * POSITIONS * CHANNELS * 2 * CHANNELS

ROUND_MAGIC = 12582912.0


def reduce_rotation_angles(nc, pool):
    one = pool.tile([P, 1], F32)
    nc.vector.memset(one[:], 1.0)
    warm = pool.tile([P, 1], F32)
    nc.scalar.activation(out=warm[:], in_=one[:], func=ACT.Sin)

    position_int = pool.tile([P, SUB], I32)
    nc.gpsimd.iota(position_int[:], pattern=[[1, SUB]], base=1, channel_multiplier=SUB)
    position = pool.tile([P, SUB], F32)
    nc.vector.tensor_copy(out=position[:], in_=position_int[:])

    ratio = 1000.0 ** (-2.0 / HEAD_DIM)
    frequency = pool.tile([P, PAIRS], F32)
    nc.vector.tensor_scalar_mul(out=frequency[:, 0:1], in0=one[:], scalar1=ratio / (2.0 * math.pi))
    half = 1
    while half < PAIRS:
        nc.vector.tensor_scalar_mul(
            out=frequency[:, half : 2 * half], in0=frequency[:, 0:half], scalar1=ratio**half
        )
        half *= 2
    plus_half_pi = pool.tile([P, 1], F32)
    nc.vector.tensor_scalar_mul(out=plus_half_pi[:], in0=one[:], scalar1=0.5 * math.pi)
    minus_half_pi = pool.tile([P, 1], F32)
    nc.vector.tensor_scalar_mul(out=minus_half_pi[:], in0=one[:], scalar1=-0.5 * math.pi)

    n = SUB * PAIRS
    turns = pool.tile([P, 2, n], F32)
    nc.vector.tensor_tensor(
        out=turns[:, 0, :].rearrange("p (i j) -> p i j", j=PAIRS),
        in0=position[:].unsqueeze(2).to_broadcast([P, SUB, PAIRS]),
        in1=frequency[:].unsqueeze(1).to_broadcast([P, SUB, PAIRS]),
        op=ALU.mult,
    )
    nc.vector.tensor_scalar_add(out=turns[:, 1, :], in0=turns[:, 0, :], scalar1=-0.25)
    whole = pool.tile([P, 2, n], F32)
    nc.vector.tensor_scalar(
        out=whole[:],
        in0=turns[:],
        scalar1=ROUND_MAGIC,
        scalar2=ROUND_MAGIC,
        op0=ALU.add,
        op1=ALU.subtract,
    )
    part = pool.tile([P, 2, n], F32)
    nc.vector.tensor_tensor(out=part[:], in0=turns[:], in1=whole[:], op=ALU.subtract)
    size = pool.tile([P, 2, n], F32)
    nc.vector.scalar_tensor_tensor(
        out=size[:], in0=part[:], scalar=-1.0, in1=part[:], op0=ALU.mult, op1=ALU.max
    )
    return size, plus_half_pi, minus_half_pi


def fill_rotation_tables(nc, size, plus_half_pi, minus_half_pi, cos_table, sin_table):
    n = SUB * PAIRS
    cos_pairs = cos_table.rearrange("p i (j e) -> p (i j) e", e=2)
    sin_pairs = sin_table.rearrange("p i (j e) -> p (i j) e", e=2)
    nc.scalar.activation(
        out=sin_pairs[:, :, 0:1],
        in_=size[:, 1, :].unsqueeze(2),
        func=ACT.Sin,
        bias=minus_half_pi[:],
        scale=2.0 * math.pi,
    )
    nc.scalar.activation(
        out=sin_pairs[:, :, 1:2],
        in_=size[:, 1, :].unsqueeze(2),
        func=ACT.Sin,
        bias=plus_half_pi[:],
        scale=-2.0 * math.pi,
    )
    nc.scalar.activation(
        out=cos_pairs,
        in_=size[:, 0, :].unsqueeze(2).to_broadcast([P, n, 2]),
        func=ACT.Sin,
        bias=plus_half_pi[:],
        scale=-2.0 * math.pi,
    )


def channels_to_partitions(nc, banks, copiers, rows, n_tiles, permutation, grouped):
    words = rows.bitcast(F32)
    grouped_words = grouped.bitcast(F32).rearrange("p (t r u) -> p t r u", r=P, u=2)
    for first in range(0, n_tiles, 2):
        bank = banks.tile([P, 2, 2, P], F32, tag="bank")
        for t in range(2):
            for u in range(2):
                start = (first + t) * WORDS + u * P
                nc.tensor.transpose(bank[:, t, u, :], words[:, start : start + P], permutation)
        copy_out = copiers[(first // 2) % len(copiers)]
        copy_out(
            out=grouped_words[:, first : first + 2, :, :],
            in_=bank[:].rearrange("p t u r -> p t r u"),
        )


def tile_ropeattnlayer_pa_t_kernel(tc, x, w_qk, out_0, out_1, out_2, out_3):
    nc = tc.nc
    raw_outs = (out_0, out_1)
    rotated_outs = (out_2, out_3)

    with ExitStack() as ctx:
        keep = ctx.enter_context(tc.tile_pool(name="keep", bufs=1))
        stage = ctx.enter_context(tc.tile_pool(name="stage", bufs=2))
        terms = ctx.enter_context(tc.tile_pool(name="terms", bufs=3))
        results = ctx.enter_context(tc.tile_pool(name="results", bufs=4))
        banks = ctx.enter_context(tc.psum_pool(name="banks", bufs=8))
        ctx.enter_context(tc.manual_schedule())

        w_rows = []
        for s in range(2):
            w_rows.append(keep.tile([P, HALF_TILES * CHANNELS], BF16, name="w_rows_%d" % s))
            nc.sync.dma_start(
                out=w_rows[s][:].rearrange("p (t c) -> p t c", c=CHANNELS),
                in_=w_qk[s * CHANNELS : (s + 1) * CHANNELS, :].rearrange("(t p) c -> p t c", p=P),
            )
        x_rows = []
        for b in range(BATCH):
            x_rows.append(keep.tile([P, SUB * CHANNELS], BF16, name="x_rows_%d" % b))
            nc.sync.dma_start(out=x_rows[b][:], in_=x[b].rearrange("(p i) c -> p (i c)", i=SUB))

        size, plus_half_pi, minus_half_pi = reduce_rotation_angles(nc, keep)

        identity = keep.tile([P, P], F32)
        make_identity(nc, identity[:])
        swap = keep.tile([P, P], F32)
        identity_pairs = identity[:].rearrange("p (m s) -> p m s", s=2)
        swap_pairs = swap[:].rearrange("p (m s) -> p m s", s=2)
        nc.vector.tensor_copy(out=swap_pairs[:, :, 0:1], in_=identity_pairs[:, :, 1:2])
        nc.vector.tensor_copy(out=swap_pairs[:, :, 1:2], in_=identity_pairs[:, :, 0:1])

        w_codes = {}
        w_scales = {}
        for s in range(2):
            for kind, permutation in (("partner", swap), ("own", identity)):
                label = "%s_%d" % (kind, s)
                w_grouped = stage.tile([P, CHANNELS * 4], BF16, name="w_grouped", align_bytes=64)
                w_codes[kind, s] = keep.tile([P, CHANNELS], U32, name="w_codes_" + label, align_bytes=64)
                w_scales[kind, s] = keep.tile([P, CHANNELS], U8, name="w_scales_" + label, align_bytes=64)
                channels_to_partitions(
                    nc, banks, (nc.scalar.copy, nc.vector.tensor_copy),
                    w_rows[s][:], HALF_TILES, permutation[:], w_grouped[:],
                )
                nc.vector.quantize_mx(
                    out=w_codes[kind, s][:].bitcast(FP8X4), scales=w_scales[kind, s][:], in_=w_grouped[:]
                )
        x_codes = []
        x_scales = []
        for b in range(BATCH):
            x_grouped = stage.tile([P, POSITIONS * 4], BF16, name="x_grouped", align_bytes=64)
            x_codes.append(keep.tile([P, POSITIONS], U32, name="x_codes_%d" % b, align_bytes=64))
            x_scales.append(keep.tile([P, POSITIONS], U8, name="x_scales_%d" % b, align_bytes=64))
            channels_to_partitions(
                nc, banks, (nc.scalar.copy,), x_rows[b][:], SUB, identity[:], x_grouped[:]
            )
            nc.vector.quantize_mx(
                out=x_codes[b][:].bitcast(FP8X4), scales=x_scales[b][:], in_=x_grouped[:]
            )

        cos_table = keep.tile([P, SUB, HEAD_DIM], F32)
        sin_table = keep.tile([P, SUB, HEAD_DIM], F32)
        fill_rotation_tables(nc, size, plus_half_pi, minus_half_pi, cos_table[:], sin_table[:])

        def store(outs, s, b, result):
            nc.sync.dma_start(
                out=outs[s][b].rearrange("h (p i) f -> p h (i f)", i=SUB),
                in_=result[:].rearrange("p h i f -> p h (i f)"),
            )

        unstored = []
        for s in range(2):
            for b in range(BATCH):
                raw = results.tile([P, HEADS, SUB, HEAD_DIM], F32, name="raw")
                rotated = results.tile([P, HEADS, SUB, HEAD_DIM], F32, name="rotated")
                straight = terms.tile([P, SUB, HEADS, HEAD_DIM], F32, name="straight")
                crossed = terms.tile([P, SUB, HEADS, HEAD_DIM], F32, name="crossed")
                for first in range(0, SUB, 2):
                    product = {}
                    for kind in ("partner", "own"):
                        for i in (first, first + 1):
                            tokens = slice(i * P, (i + 1) * P)
                            product[kind, i] = banks.tile([P, HEADS, HEAD_DIM], F32, tag="bank", name="product")
                            nc.tensor.matmul_mx(
                                out=product[kind, i][:].rearrange("p h f -> p (h f)"),
                                lhsT=x_codes[b][:, tokens].bitcast(FP8X4),
                                lhsT_scale=x_scales[b][:, tokens],
                                rhs=w_codes[kind, s][:].bitcast(FP8X4),
                                rhs_scale=w_scales[kind, s][:],
                                start=True,
                                stop=True,
                            )
                    for i in (first, first + 1):
                        nc.scalar.copy(out=raw[:, :, i, :], in_=product["own", i][:])
                        nc.vector.tensor_tensor(
                            out=crossed[:, i, :, :],
                            in0=product["partner", i][:],
                            in1=sin_table[:, i : i + 1, :].to_broadcast([P, HEADS, HEAD_DIM]),
                            op=ALU.mult,
                        )
                    for i in (first, first + 1):
                        nc.vector.tensor_tensor(
                            out=straight[:, i, :, :],
                            in0=product["own", i][:],
                            in1=cos_table[:, i : i + 1, :].to_broadcast([P, HEADS, HEAD_DIM]),
                            op=ALU.mult,
                        )
                last_step = s == 1 and b == BATCH - 1
                adder = nc.vector if last_step else nc.gpsimd
                adder.tensor_tensor(
                    out=rotated[:],
                    in0=straight[:].rearrange("p i h f -> p h i f"),
                    in1=crossed[:].rearrange("p i h f -> p h i f"),
                    op=ALU.add,
                )
                store(raw_outs, s, b, raw)
                for earlier in unstored:
                    store(rotated_outs, *earlier)
                unstored = [(s, b, rotated)]
        for earlier in unstored:
            store(rotated_outs, *earlier)
